import numpy as np
import ml_dtypes


def mxq(x, axis, fmt="e4m3"):
    dtype, down = {"e4m3": (ml_dtypes.float8_e4m3fn, 7), "e5m2": (ml_dtypes.float8_e5m2, 14)}[fmt]
    v = np.moveaxis(np.asarray(x, np.float32).astype(ml_dtypes.bfloat16).astype(np.float64), axis, -1)
    blocks = v.reshape(v.shape[:-1] + (-1, 32))
    amax = np.abs(blocks).max(-1, keepdims=True)
    byte = np.maximum(np.where(amax > 0, np.frexp(amax)[1] - 1 + 127, 0) - down, 1)
    scale = np.exp2(byte - 127.0)
    codes = (blocks / scale).astype(np.float32).astype(dtype).astype(np.float64)
    return np.moveaxis((codes * scale).reshape(v.shape), -1, axis)


WIDE = False


def mx_kscale(k):
    if not WIDE:
        return np.ones(k)
    levels = np.array([10, -10, 5, -5, 0])
    a = np.random.permutation(np.resize(levels, k // 512 * 4)).reshape(k // 512, 4)
    idx = np.arange(k)
    return np.exp2(a[idx // 512, idx % 128 // 32])


BF16 = ml_dtypes.bfloat16


def bf(x):
    return np.asarray(x, np.float32).astype(BF16)


def f64(x):
    return np.asarray(x).astype(np.float64)


N, S, D, H, O = 4, 1024, 1024, 512, 1024


def elu(v):
    return np.where(v > 0.0, v, np.exp(np.minimum(v, 0.0)) - 1.0)


def setup_inputs():
    s = mx_kscale(D)
    return {"x": bf(np.random.standard_normal((N, S, D)) * s),
            "Wk": bf(np.random.standard_normal((D, H)) / np.sqrt(D) / s[:, None]),
            "bk": bf(np.random.standard_normal(H) * 0.1),
            "Wv": bf(np.random.standard_normal((D, H)) / np.sqrt(D) / s[:, None]),
            "bv": bf(np.random.standard_normal(H) * 0.1)}


def reference(x, Wk, bk, Wv, bv):
    xq = mxq(f64(x), 2, "e4m3")
    keyp = (xq @ mxq(f64(Wk), 0, "e4m3")) + f64(bk)
    value = (xq @ mxq(f64(Wv), 0, "e4m3")) + f64(bv)
    K = elu(keyp) + 1.0
    KV = np.sum(K * value, axis=1)
    Ksum = np.sum(K, axis=1)
    return KV, Ksum

@@ -1,0 +1,242 @@
+from contextlib import ExitStack
+
+import concourse.mybir as mybir
+from concourse.masks import make_identity
+
+F32 = mybir.dt.float32
+BF16 = mybir.dt.bfloat16
+U32 = mybir.dt.uint32
+U8 = mybir.dt.uint8
+FP8X4 = mybir.dt.float8_e4m3fn_x4
+ACT = mybir.ActivationFunctionType
+ALU = mybir.AluOpType
+AXIS = mybir.AxisListType
+
+P = 128
+PACK = 4
+BATCH, SEQ, D, H = 4, 1024, 1024, 512
+PASSES = D // (P * PACK)
+CHUNK = 512
+CHUNKS = BATCH * SEQ // CHUNK
+CHUNKS_PER_BATCH = SEQ // CHUNK
+ROWS = CHUNK // P
+WORDS = D // 2
+H_TILES = H // P
+UNITS = CHUNKS * PASSES
+STEP_TILES = 2
+STEPS = CHUNKS * H_TILES // STEP_TILES
+
+FLOPS = 2 * BATCH * SEQ * D * (2 * H)
+
+
+def tile_linearattention_pa_t_kernel(tc, x, Wk, bk, Wv, bv, out_0, out_1):
+    nc = tc.nc
+    with ExitStack() as ctx:
+        ctx.enter_context(tc.manual_schedule())
+        const = ctx.enter_context(tc.tile_pool(name="const", bufs=1))
+        x_pool = ctx.enter_context(tc.tile_pool(name="x", bufs=1))
+        w_pool = ctx.enter_context(tc.tile_pool(name="w", bufs=1))
+        xq_pool = ctx.enter_context(tc.tile_pool(name="xq", bufs=2))
+        work = ctx.enter_context(tc.tile_pool(name="work", bufs=4))
+        psum_t = ctx.enter_context(tc.psum_pool(name="psum_t", bufs=2))
+        psum_k = ctx.enter_context(tc.psum_pool(name="psum_k", bufs=4))
+        psum_v = ctx.enter_context(tc.psum_pool(name="psum_v", bufs=2))
+
+        x_chunks = x.flatten_outer_dims().rearrange("(c p r) d -> c p (r d)", p=P, r=ROWS)
+        x_tiles = [x_pool.tile([P, ROWS * D], BF16, name="x%d" % c) for c in range(CHUNKS)]
+
+        def load_weight(w, label):
+            raw = w_pool.tile([P, PASSES * PACK, H], BF16, name="raw_" + label)
+            nc.sync.dma_start(
+                out=raw[:].rearrange("p (q e) h -> p q (e h)", e=2),
+                in_=w.rearrange("(q p e) h -> p q (e h)", p=P, e=2),
+            )
+            return raw
+
+        nc.sync.dma_start(out=x_tiles[0][:], in_=x_chunks[0])
+        raw_k = load_weight(Wk, "k")
+        raw_v = load_weight(Wv, "v")
+        for c in range(1, CHUNKS):
+            nc.sync.dma_start(out=x_tiles[c][:], in_=x_chunks[c])
+
+        ident = const.tile([P, P], F32)
+        make_identity(nc, ident[:])
+
+        bias_rows = const.tile([P, P], BF16)
+        nc.vector.memset(bias_rows[:], 0.0)
+        nc.scalar.dma_start(out=bias_rows[0:H_TILES, :], in_=bk.rearrange("(j h) -> j h", h=P))
+        nc.scalar.dma_start(out=bias_rows[H_TILES : 2 * H_TILES, :], in_=bv.rearrange("(j h) -> j h", h=P))
+        warm = const.tile([P, 2], F32)
+        nc.vector.memset(warm[:], 0.0)
+        nc.scalar.activation(out=warm[:, 1:2], in_=warm[:, 0:1], func=ACT.Exp)
+        totals = const.tile([P, P], F32)
+        nc.vector.memset(totals[:], 0.0)
+        bias_rows_f32 = const.tile([P, P], F32)
+        nc.vector.tensor_copy(out=bias_rows_f32[:], in_=bias_rows[:])
+        bias_bank = psum_t.tile([P, P], F32, tag="t")
+        nc.tensor.transpose(bias_bank[:], bias_rows_f32[:], ident[:])
+        bias = const.tile([P, 2 * H_TILES], F32)
+        nc.vector.tensor_copy(out=bias[:], in_=bias_bank[:, 0 : 2 * H_TILES])
+        bk_plus_1 = const.tile([P, H_TILES], F32)
+        nc.vector.tensor_scalar_add(out=bk_plus_1[:], in0=bias[:, 0:H_TILES], scalar1=1.0)
+
+        ksum_parts = const.tile([P, BATCH * H_TILES * CHUNKS_PER_BATCH], F32)
+        kv_parts = const.tile([P, BATCH * H_TILES * CHUNKS_PER_BATCH], F32)
+
+        def regroup_weight(raw, label):
+            grouped = w_pool.tile([P, PASSES * H * PACK], BF16, name="grouped_" + label, align_bytes=64)
+            for g in range(PASSES):
+                nc.vector.tensor_copy(
+                    out=grouped[:, g * H * PACK : (g + 1) * H * PACK].rearrange(
+                        "p (c i t) -> p c t i", i=4, t=PACK
+                    ),
+                    in_=raw[:, g * PACK : (g + 1) * PACK, :].rearrange("p t (c i) -> p c t i", i=4),
+                )
+            return grouped
+
+        def quantise_weight(grouped, label):
+            codes = w_pool.tile([P, PASSES * H], U32, name="codes_" + label, align_bytes=64)
+            scales = w_pool.tile([P, PASSES * H], U8, name="scales_" + label, align_bytes=64)
+            nc.vector.quantize_mx(out=codes[:].bitcast(FP8X4), scales=scales[:], in_=grouped[:])
+            return codes, scales
+
+        grouped_x = {}
+        x_codes = {}
+
+        def transpose_unit(unit):
+            c, g = divmod(unit, PASSES)
+            if g == 0:
+                grouped_x[c] = xq_pool.tile([P, PASSES * CHUNK * PACK], BF16, name="grouped_x", align_bytes=64)
+            words_in = x_tiles[c][:].bitcast(F32)
+            words_out = grouped_x[c][:].bitcast(F32)
+            for half in range(2):
+                bank = psum_t.tile([P, 2, 2 * P], F32, tag="t")
+                for u in range(2):
+                    for r in range(2):
+                        first = (2 * half + r) * WORDS + (2 * g + u) * P
+                        nc.tensor.transpose(
+                            bank[:, u, r * P : (r + 1) * P], words_in[:, first : first + P], ident[:]
+                        )
+                start = 2 * (g * CHUNK + half * 2 * P)
+                nc.scalar.copy(
+                    out=words_out[:, start : start + 4 * P].rearrange("p (s u) -> p s u", u=2),
+                    in_=bank[:].rearrange("p u s -> p s u"),
+                )
+
+        def quantise_chunk(c):
+            codes = xq_pool.tile([P, PASSES * CHUNK], U32, name="codes_x", align_bytes=64)
+            scales = xq_pool.tile([P, PASSES * CHUNK], U8, name="scales_x", align_bytes=64)
+            nc.vector.quantize_mx(out=codes[:].bitcast(FP8X4), scales=scales[:], in_=grouped_x[c][:])
+            x_codes[c] = (codes, scales)
+
+        def product(bank, weight, c, j):
+            w_codes, w_scales = weight
+            codes, scales = x_codes[c]
+            for g in range(PASSES):
+                w_cols = slice(g * H + j * P, g * H + (j + 1) * P)
+                x_cols = slice(g * CHUNK, (g + 1) * CHUNK)
+                nc.tensor.matmul_mx(
+                    out=bank[:],
+                    lhsT=w_codes[:, w_cols].bitcast(FP8X4),
+                    lhsT_scale=w_scales[:, w_cols],
+                    rhs=codes[:, x_cols].bitcast(FP8X4),
+                    rhs_scale=scales[:, x_cols],
+                    start=(g == 0),
+                    stop=(g == PASSES - 1),
+                )
+
+        def blocks_of(step):
+            c, part = divmod(step, H_TILES // STEP_TILES)
+            return c, range(part * STEP_TILES, (part + 1) * STEP_TILES)
+
+        def part_column(c, j):
+            n, chunk_of_batch = divmod(c, CHUNKS_PER_BATCH)
+            return (n * H_TILES + j) * CHUNKS_PER_BATCH + chunk_of_batch
+
+        key_banks = {}
+        small_exps = {}
+
+        def key_stage(step):
+            c, blocks = blocks_of(step)
+            for j in blocks:
+                key_bank = psum_k.tile([P, CHUNK], F32, tag="k")
+                product(key_bank, weight_k, c, j)
+                small_exp = work.tile([P, CHUNK], F32, tag="small_exp")
+                nc.scalar.activation(out=small_exp[:], in_=key_bank[:], func=ACT.Exp, bias=bias[:, j : j + 1])
+                nc.gpsimd.tensor_scalar(
+                    out=small_exp[:], in0=small_exp[:], scalar1=1.0, scalar2=0.0, op0=ALU.min, op1=ALU.max
+                )
+                key_banks[(c, j)] = key_bank
+                small_exps[(c, j)] = small_exp
+
+        def value_stage(step):
+            c, blocks = blocks_of(step)
+            value_banks = {}
+            features = {}
+            for j in blocks:
+                value_banks[j] = psum_v.tile([P, CHUNK], F32, tag="v", name="value_bank")
+                product(value_banks[j], weight_v, c, j)
+            for j in blocks:
+                column = part_column(c, j)
+                features[j] = work.tile([P, CHUNK], F32, tag="feature", name="feature")
+                nc.vector.scalar_tensor_tensor(
+                    out=features[j][:],
+                    in0=key_banks[(c, j)][:],
+                    scalar=bk_plus_1[:, j : j + 1],
+                    in1=small_exps[(c, j)][:],
+                    op0=ALU.add,
+                    op1=ALU.max,
+                    accum_out=ksum_parts[:, column : column + 1],
+                )
+            for j in blocks:
+                column = part_column(c, j)
+                weighted = work.tile([P, CHUNK], F32, tag="weighted")
+                nc.vector.scalar_tensor_tensor(
+                    out=weighted[:],
+                    in0=value_banks[j][:],
+                    scalar=bias[:, H_TILES + j : H_TILES + j + 1],
+                    in1=features[j][:],
+                    op0=ALU.add,
+                    op1=ALU.mult,
+                    accum_out=kv_parts[:, column : column + 1],
+                )
+
+        transpose_unit(0)
+        transpose_unit(1)
+        grouped_k = regroup_weight(raw_k, "k")
+        quantise_chunk(0)
+        weight_k = quantise_weight(grouped_k, "k")
+        transpose_unit(2)
+        key_stage(0)
+        transpose_unit(3)
+        grouped_v = regroup_weight(raw_v, "v")
+        weight_v = quantise_weight(grouped_v, "v")
+        for step in range(STEPS):
+            if step + 1 < STEPS:
+                key_stage(step + 1)
+            if step + 4 < UNITS:
+                transpose_unit(step + 4)
+            value_stage(step)
+            next_chunk = step // 2 + 1
+            if step % 2 == 0 and next_chunk < CHUNKS:
+                quantise_chunk(next_chunk)
+
+        results = BATCH * H_TILES
+        nc.vector.tensor_reduce(
+            out=totals[:, 0:results],
+            in_=kv_parts[:].rearrange("p (r k) -> p r k", k=CHUNKS_PER_BATCH),
+            axis=AXIS.X,
+            op=ALU.add,
+        )
+        nc.vector.tensor_reduce(
+            out=totals[:, results : 2 * results],
+            in_=ksum_parts[:].rearrange("p (r k) -> p r k", k=CHUNKS_PER_BATCH),
+            axis=AXIS.X,
+            op=ALU.add,
+        )
+        totals_bank = psum_t.tile([P, P], F32, tag="t")
+        nc.tensor.transpose(totals_bank[:], totals[:], ident[:])
+        rows = const.tile([P, P], F32)
+        nc.vector.tensor_copy(out=rows[:], in_=totals_bank[:])
+        nc.sync.dma_start(out=out_0.rearrange("n (j h) -> (n j) h", h=P), in_=rows[0:results, :])
+        nc.sync.dma_start(out=out_1.rearrange("n (j h) -> (n j) h", h=P), in_=rows[results : 2 * results, :])

@@ -53,6 +53,10 @@ def tile_linearattention_pa_t_kernel(tc, x, Wk, bk, Wv, bv, out_0, out_1):
             )
             return raw
 
+        bias_rows = const.tile([P, P], BF16)
+        nc.vector.memset(bias_rows[:], 0.0)
+        nc.sync.dma_start(out=bias_rows[0:H_TILES, :], in_=bk.rearrange("(j h) -> j h", h=P))
+        nc.sync.dma_start(out=bias_rows[H_TILES : 2 * H_TILES, :], in_=bv.rearrange("(j h) -> j h", h=P))
         nc.sync.dma_start(out=x_tiles[0][:], in_=x_chunks[0])
         raw_k = load_weight(Wk, "k")
         raw_v = load_weight(Wv, "v")
@@ -62,10 +66,6 @@ def tile_linearattention_pa_t_kernel(tc, x, Wk, bk, Wv, bv, out_0, out_1):
         ident = const.tile([P, P], F32)
         make_identity(nc, ident[:])
 
-        bias_rows = const.tile([P, P], BF16)
-        nc.vector.memset(bias_rows[:], 0.0)
-        nc.scalar.dma_start(out=bias_rows[0:H_TILES, :], in_=bk.rearrange("(j h) -> j h", h=P))
-        nc.scalar.dma_start(out=bias_rows[H_TILES : 2 * H_TILES, :], in_=bv.rearrange("(j h) -> j h", h=P))
         warm = const.tile([P, 2], F32)
         nc.vector.memset(warm[:], 0.0)
         nc.scalar.activation(out=warm[:, 1:2], in_=warm[:, 0:1], func=ACT.Exp)
@@ -159,15 +159,17 @@ def tile_linearattention_pa_t_kernel(tc, x, Wk, bk, Wv, bv, out_0, out_1):
         def key_stage(step):
             c, blocks = blocks_of(step)
             for j in blocks:
-                key_bank = psum_k.tile([P, CHUNK], F32, tag="k")
-                product(key_bank, weight_k, c, j)
-                small_exp = work.tile([P, CHUNK], F32, tag="small_exp")
-                nc.scalar.activation(out=small_exp[:], in_=key_bank[:], func=ACT.Exp, bias=bias[:, j : j + 1])
-                nc.gpsimd.tensor_scalar(
-                    out=small_exp[:], in0=small_exp[:], scalar1=1.0, scalar2=0.0, op0=ALU.min, op1=ALU.max
+                key_banks[(c, j)] = psum_k.tile([P, CHUNK], F32, tag="k", name="key_bank")
+                product(key_banks[(c, j)], weight_k, c, j)
+            for j in blocks:
+                small_exps[(c, j)] = work.tile([P, CHUNK], F32, tag="small_exp", name="small_exp")
+                nc.scalar.activation(
+                    out=small_exps[(c, j)][:], in_=key_banks[(c, j)][:], func=ACT.Abs, bias=bias[:, j : j + 1]
                 )
-                key_banks[(c, j)] = key_bank
-                small_exps[(c, j)] = small_exp
+            for j in blocks:
+                nc.scalar.activation(
+                    out=small_exps[(c, j)][:], in_=small_exps[(c, j)][:], func=ACT.Exp, scale=-1.0
+                )
 
         def value_stage(step):
             c, blocks = blocks_of(step)

@@ -59,8 +59,9 @@ def tile_linearattention_pa_t_kernel(tc, x, Wk, bk, Wv, bv, out_0, out_1):
         nc.sync.dma_start(out=bias_rows[H_TILES : 2 * H_TILES, :], in_=bv.rearrange("(j h) -> j h", h=P))
         nc.sync.dma_start(out=x_tiles[0][:], in_=x_chunks[0])
         raw_k = load_weight(Wk, "k")
+        nc.sync.dma_start(out=x_tiles[1][:], in_=x_chunks[1])
         raw_v = load_weight(Wv, "v")
-        for c in range(1, CHUNKS):
+        for c in range(2, CHUNKS):
             nc.sync.dma_start(out=x_tiles[c][:], in_=x_chunks[c])
 
         ident = const.tile([P, P], F32)
@@ -209,19 +210,20 @@ def tile_linearattention_pa_t_kernel(tc, x, Wk, bk, Wv, bv, out_0, out_1):
         quantise_chunk(0)
         weight_k = quantise_weight(grouped_k, "k")
         transpose_unit(2)
-        key_stage(0)
         transpose_unit(3)
+        key_stage(0)
         grouped_v = regroup_weight(raw_v, "v")
         weight_v = quantise_weight(grouped_v, "v")
+        steps_per_chunk = H_TILES // STEP_TILES
         for step in range(STEPS):
-            if step + 1 < STEPS:
-                key_stage(step + 1)
+            next_chunk = step // steps_per_chunk + 1
+            if step % steps_per_chunk == 0 and next_chunk < CHUNKS:
+                quantise_chunk(next_chunk)
             if step + 4 < UNITS:
                 transpose_unit(step + 4)
+            if step + 1 < STEPS:
+                key_stage(step + 1)
             value_stage(step)
-            next_chunk = step // 2 + 1
-            if step % 2 == 0 and next_chunk < CHUNKS:
-                quantise_chunk(next_chunk)
 
         results = BATCH * H_TILES
         nc.vector.tensor_reduce(

@@ -165,11 +165,15 @@ def tile_linearattention_pa_t_kernel(tc, x, Wk, bk, Wv, bv, out_0, out_1):
             for j in blocks:
                 small_exps[(c, j)] = work.tile([P, CHUNK], F32, tag="small_exp", name="small_exp")
                 nc.scalar.activation(
-                    out=small_exps[(c, j)][:], in_=key_banks[(c, j)][:], func=ACT.Abs, bias=bias[:, j : j + 1]
+                    out=small_exps[(c, j)][:], in_=key_banks[(c, j)][:], func=ACT.Exp, bias=bias[:, j : j + 1]
                 )
-            for j in blocks:
-                nc.scalar.activation(
-                    out=small_exps[(c, j)][:], in_=small_exps[(c, j)][:], func=ACT.Exp, scale=-1.0
+                nc.gpsimd.tensor_scalar(
+                    out=small_exps[(c, j)][:],
+                    in0=small_exps[(c, j)][:],
+                    scalar1=1.0,
+                    scalar2=0.0,
+                    op0=ALU.min,
+                    op1=ALU.max,
                 )
 
         def value_stage(step):

@@ -47,17 +47,18 @@ def tile_linearattention_pa_t_kernel(tc, x, Wk, bk, Wv, bv, out_0, out_1):
 
         def load_weight(w, label):
             raw = w_pool.tile([P, PASSES * PACK, H], BF16, name="raw_" + label)
-            nc.sync.dma_start(
-                out=raw[:].rearrange("p (q e) h -> p q (e h)", e=2),
-                in_=w.rearrange("(q p e) h -> p q (e h)", p=P, e=2),
-            )
+            for g in range(PASSES):
+                nc.sync.dma_start(
+                    out=raw[:, g * PACK : (g + 1) * PACK, :].rearrange("p (u e) h -> p u (e h)", e=2),
+                    in_=w[g * P * PACK : (g + 1) * P * PACK, :].rearrange("(u p e) h -> p u (e h)", p=P, e=2),
+                )
             return raw
 
         bias_rows = const.tile([P, P], BF16)
         nc.vector.memset(bias_rows[:], 0.0)
+        nc.sync.dma_start(out=x_tiles[0][:], in_=x_chunks[0])
         nc.sync.dma_start(out=bias_rows[0:H_TILES, :], in_=bk.rearrange("(j h) -> j h", h=P))
         nc.sync.dma_start(out=bias_rows[H_TILES : 2 * H_TILES, :], in_=bv.rearrange("(j h) -> j h", h=P))
-        nc.sync.dma_start(out=x_tiles[0][:], in_=x_chunks[0])
         raw_k = load_weight(Wk, "k")
         nc.sync.dma_start(out=x_tiles[1][:], in_=x_chunks[1])
         raw_v = load_weight(Wv, "v")
@@ -74,15 +75,16 @@ def tile_linearattention_pa_t_kernel(tc, x, Wk, bk, Wv, bv, out_0, out_1):
         nc.vector.memset(totals[:], 0.0)
         bias_rows_f32 = const.tile([P, P], F32)
         nc.vector.tensor_copy(out=bias_rows_f32[:], in_=bias_rows[:])
-        bias_bank = psum_t.tile([P, P], F32, tag="t")
-        nc.tensor.transpose(bias_bank[:], bias_rows_f32[:], ident[:])
         bias = const.tile([P, 2 * H_TILES], F32)
-        nc.vector.tensor_copy(out=bias[:], in_=bias_bank[:, 0 : 2 * H_TILES])
         bk_plus_1 = const.tile([P, H_TILES], F32)
-        nc.vector.tensor_scalar_add(out=bk_plus_1[:], in0=bias[:, 0:H_TILES], scalar1=1.0)
 
-        ksum_parts = const.tile([P, BATCH * H_TILES * CHUNKS_PER_BATCH], F32)
-        kv_parts = const.tile([P, BATCH * H_TILES * CHUNKS_PER_BATCH], F32)
+        def spread_biases():
+            bias_bank = psum_t.tile([P, P], F32, tag="t")
+            nc.tensor.transpose(bias_bank[:], bias_rows_f32[:], ident[:])
+            nc.vector.tensor_copy(out=bias[:], in_=bias_bank[:, 0 : 2 * H_TILES])
+            nc.vector.tensor_scalar_add(out=bk_plus_1[:], in0=bias[:, 0:H_TILES], scalar1=1.0)
+
+        parts = const.tile([P, 2, BATCH * H_TILES * CHUNKS_PER_BATCH], F32)
 
         def regroup_weight(raw, label):
             grouped = w_pool.tile([P, PASSES * H * PACK], BF16, name="grouped_" + label, align_bytes=64)
@@ -193,7 +195,7 @@ def tile_linearattention_pa_t_kernel(tc, x, Wk, bk, Wv, bv, out_0, out_1):
                     in1=small_exps[(c, j)][:],
                     op0=ALU.add,
                     op1=ALU.max,
-                    accum_out=ksum_parts[:, column : column + 1],
+                    accum_out=parts[:, 1, column : column + 1],
                 )
             for j in blocks:
                 column = part_column(c, j)
@@ -205,14 +207,15 @@ def tile_linearattention_pa_t_kernel(tc, x, Wk, bk, Wv, bv, out_0, out_1):
                     in1=features[j][:],
                     op0=ALU.add,
                     op1=ALU.mult,
-                    accum_out=kv_parts[:, column : column + 1],
+                    accum_out=parts[:, 0, column : column + 1],
                 )
 
         transpose_unit(0)
         transpose_unit(1)
         grouped_k = regroup_weight(raw_k, "k")
-        quantise_chunk(0)
+        spread_biases()
         weight_k = quantise_weight(grouped_k, "k")
+        quantise_chunk(0)
         transpose_unit(2)
         transpose_unit(3)
         key_stage(0)
@@ -231,14 +234,8 @@ def tile_linearattention_pa_t_kernel(tc, x, Wk, bk, Wv, bv, out_0, out_1):
 
         results = BATCH * H_TILES
         nc.vector.tensor_reduce(
-            out=totals[:, 0:results],
-            in_=kv_parts[:].rearrange("p (r k) -> p r k", k=CHUNKS_PER_BATCH),
-            axis=AXIS.X,
-            op=ALU.add,
-        )
-        nc.vector.tensor_reduce(
-            out=totals[:, results : 2 * results],
-            in_=ksum_parts[:].rearrange("p (r k) -> p r k", k=CHUNKS_PER_BATCH),
+            out=totals[:, 0 : 2 * results],
+            in_=parts[:].rearrange("p w (r k) -> p (w r) k", k=CHUNKS_PER_BATCH),
             axis=AXIS.X,
             op=ALU.add,
         )

from contextlib import ExitStack

import concourse.mybir as mybir
from concourse.masks import make_identity

F32 = mybir.dt.float32
BF16 = mybir.dt.bfloat16
U32 = mybir.dt.uint32
U8 = mybir.dt.uint8
FP8X4 = mybir.dt.float8_e4m3fn_x4
ACT = mybir.ActivationFunctionType
ALU = mybir.AluOpType
AXIS = mybir.AxisListType

P = 128
PACK = 4
BATCH, SEQ, D, H = 4, 1024, 1024, 512
PASSES = D // (P * PACK)
CHUNK = 512
CHUNKS = BATCH * SEQ // CHUNK
CHUNKS_PER_BATCH = SEQ // CHUNK
ROWS = CHUNK // P
WORDS = D // 2
H_TILES = H // P
UNITS = CHUNKS * PASSES
STEP_TILES = 2
STEPS = CHUNKS * H_TILES // STEP_TILES

FLOPS = 2 * BATCH * SEQ * D * (2 * H)


def tile_linearattention_pa_t_kernel(tc, x, Wk, bk, Wv, bv, out_0, out_1):
    nc = tc.nc
    with ExitStack() as ctx:
        ctx.enter_context(tc.manual_schedule())
        const = ctx.enter_context(tc.tile_pool(name="const", bufs=1))
        x_pool = ctx.enter_context(tc.tile_pool(name="x", bufs=1))
        w_pool = ctx.enter_context(tc.tile_pool(name="w", bufs=1))
        xq_pool = ctx.enter_context(tc.tile_pool(name="xq", bufs=2))
        work = ctx.enter_context(tc.tile_pool(name="work", bufs=4))
        psum_t = ctx.enter_context(tc.psum_pool(name="psum_t", bufs=2))
        psum_k = ctx.enter_context(tc.psum_pool(name="psum_k", bufs=4))
        psum_v = ctx.enter_context(tc.psum_pool(name="psum_v", bufs=2))

        x_chunks = x.flatten_outer_dims().rearrange("(c p r) d -> c p (r d)", p=P, r=ROWS)
        x_tiles = [x_pool.tile([P, ROWS * D], BF16, name="x%d" % c) for c in range(CHUNKS)]

        def load_weight(w, label):
            raw = w_pool.tile([P, PASSES * PACK, H], BF16, name="raw_" + label)
            for g in range(PASSES):
                nc.sync.dma_start(
                    out=raw[:, g * PACK : (g + 1) * PACK, :].rearrange("p (u e) h -> p u (e h)", e=2),
                    in_=w[g * P * PACK : (g + 1) * P * PACK, :].rearrange("(u p e) h -> p u (e h)", p=P, e=2),
                )
            return raw

        bias_rows = const.tile([P, P], BF16)
        nc.vector.memset(bias_rows[:], 0.0)
        nc.sync.dma_start(out=x_tiles[0][:], in_=x_chunks[0])
        nc.sync.dma_start(out=bias_rows[0:H_TILES, :], in_=bk.rearrange("(j h) -> j h", h=P))
        nc.sync.dma_start(out=bias_rows[H_TILES : 2 * H_TILES, :], in_=bv.rearrange("(j h) -> j h", h=P))
        raw_k = load_weight(Wk, "k")
        nc.sync.dma_start(out=x_tiles[1][:], in_=x_chunks[1])
        raw_v = load_weight(Wv, "v")
        for c in range(2, CHUNKS):
            nc.sync.dma_start(out=x_tiles[c][:], in_=x_chunks[c])

        ident = const.tile([P, P], F32)
        make_identity(nc, ident[:])

        warm = const.tile([P, 2], F32)
        nc.vector.memset(warm[:], 0.0)
        nc.scalar.activation(out=warm[:, 1:2], in_=warm[:, 0:1], func=ACT.Exp)
        totals = const.tile([P, P], F32)
        nc.vector.memset(totals[:], 0.0)
        bias_rows_f32 = const.tile([P, P], F32)
        nc.vector.tensor_copy(out=bias_rows_f32[:], in_=bias_rows[:])
        bias = const.tile([P, 2 * H_TILES], F32)
        bk_plus_1 = const.tile([P, H_TILES], F32)

        def spread_biases():
            bias_bank = psum_t.tile([P, P], F32, tag="t")
            nc.tensor.transpose(bias_bank[:], bias_rows_f32[:], ident[:])
            nc.vector.tensor_copy(out=bias[:], in_=bias_bank[:, 0 : 2 * H_TILES])
            nc.vector.tensor_scalar_add(out=bk_plus_1[:], in0=bias[:, 0:H_TILES], scalar1=1.0)

        parts = const.tile([P, 2, BATCH * H_TILES * CHUNKS_PER_BATCH], F32)

        def regroup_weight(raw, label):
            grouped = w_pool.tile([P, PASSES * H * PACK], BF16, name="grouped_" + label, align_bytes=64)
            for g in range(PASSES):
                nc.vector.tensor_copy(
                    out=grouped[:, g * H * PACK : (g + 1) * H * PACK].rearrange(
                        "p (c i t) -> p c t i", i=4, t=PACK
                    ),
                    in_=raw[:, g * PACK : (g + 1) * PACK, :].rearrange("p t (c i) -> p c t i", i=4),
                )
            return grouped

        def quantise_weight(grouped, label):
            codes = w_pool.tile([P, PASSES * H], U32, name="codes_" + label, align_bytes=64)
            scales = w_pool.tile([P, PASSES * H], U8, name="scales_" + label, align_bytes=64)
            nc.vector.quantize_mx(out=codes[:].bitcast(FP8X4), scales=scales[:], in_=grouped[:])
            return codes, scales

        grouped_x = {}
        x_codes = {}

        def transpose_unit(unit):
            c, g = divmod(unit, PASSES)
            if g == 0:
                grouped_x[c] = xq_pool.tile([P, PASSES * CHUNK * PACK], BF16, name="grouped_x", align_bytes=64)
            words_in = x_tiles[c][:].bitcast(F32)
            words_out = grouped_x[c][:].bitcast(F32)
            for half in range(2):
                bank = psum_t.tile([P, 2, 2 * P], F32, tag="t")
                for u in range(2):
                    for r in range(2):
                        first = (2 * half + r) * WORDS + (2 * g + u) * P
                        nc.tensor.transpose(
                            bank[:, u, r * P : (r + 1) * P], words_in[:, first : first + P], ident[:]
                        )
                start = 2 * (g * CHUNK + half * 2 * P)
                nc.scalar.copy(
                    out=words_out[:, start : start + 4 * P].rearrange("p (s u) -> p s u", u=2),
                    in_=bank[:].rearrange("p u s -> p s u"),
                )

        def quantise_chunk(c):
            codes = xq_pool.tile([P, PASSES * CHUNK], U32, name="codes_x", align_bytes=64)
            scales = xq_pool.tile([P, PASSES * CHUNK], U8, name="scales_x", align_bytes=64)
            nc.vector.quantize_mx(out=codes[:].bitcast(FP8X4), scales=scales[:], in_=grouped_x[c][:])
            x_codes[c] = (codes, scales)

        def product(bank, weight, c, j):
            w_codes, w_scales = weight
            codes, scales = x_codes[c]
            for g in range(PASSES):
                w_cols = slice(g * H + j * P, g * H + (j + 1) * P)
                x_cols = slice(g * CHUNK, (g + 1) * CHUNK)
                nc.tensor.matmul_mx(
                    out=bank[:],
                    lhsT=w_codes[:, w_cols].bitcast(FP8X4),
                    lhsT_scale=w_scales[:, w_cols],
                    rhs=codes[:, x_cols].bitcast(FP8X4),
                    rhs_scale=scales[:, x_cols],
                    start=(g == 0),
                    stop=(g == PASSES - 1),
                )

        def blocks_of(step):
            c, part = divmod(step, H_TILES // STEP_TILES)
            return c, range(part * STEP_TILES, (part + 1) * STEP_TILES)

        def part_column(c, j):
            n, chunk_of_batch = divmod(c, CHUNKS_PER_BATCH)
            return (n * H_TILES + j) * CHUNKS_PER_BATCH + chunk_of_batch

        key_banks = {}
        small_exps = {}

        def key_stage(step):
            c, blocks = blocks_of(step)
            for j in blocks:
                key_banks[(c, j)] = psum_k.tile([P, CHUNK], F32, tag="k", name="key_bank")
                product(key_banks[(c, j)], weight_k, c, j)
            for j in blocks:
                small_exps[(c, j)] = work.tile([P, CHUNK], F32, tag="small_exp", name="small_exp")
                nc.scalar.activation(
                    out=small_exps[(c, j)][:], in_=key_banks[(c, j)][:], func=ACT.Exp, bias=bias[:, j : j + 1]
                )
                nc.gpsimd.tensor_scalar(
                    out=small_exps[(c, j)][:],
                    in0=small_exps[(c, j)][:],
                    scalar1=1.0,
                    scalar2=0.0,
                    op0=ALU.min,
                    op1=ALU.max,
                )

        def value_stage(step):
            c, blocks = blocks_of(step)
            value_banks = {}
            features = {}
            for j in blocks:
                value_banks[j] = psum_v.tile([P, CHUNK], F32, tag="v", name="value_bank")
                product(value_banks[j], weight_v, c, j)
            for j in blocks:
                column = part_column(c, j)
                features[j] = work.tile([P, CHUNK], F32, tag="feature", name="feature")
                nc.vector.scalar_tensor_tensor(
                    out=features[j][:],
                    in0=key_banks[(c, j)][:],
                    scalar=bk_plus_1[:, j : j + 1],
                    in1=small_exps[(c, j)][:],
                    op0=ALU.add,
                    op1=ALU.max,
                    accum_out=parts[:, 1, column : column + 1],
                )
            for j in blocks:
                column = part_column(c, j)
                weighted = work.tile([P, CHUNK], F32, tag="weighted")
                nc.vector.scalar_tensor_tensor(
                    out=weighted[:],
                    in0=value_banks[j][:],
                    scalar=bias[:, H_TILES + j : H_TILES + j + 1],
                    in1=features[j][:],
                    op0=ALU.add,
                    op1=ALU.mult,
                    accum_out=parts[:, 0, column : column + 1],
                )

        transpose_unit(0)
        transpose_unit(1)
        grouped_k = regroup_weight(raw_k, "k")
        spread_biases()
        weight_k = quantise_weight(grouped_k, "k")
        quantise_chunk(0)
        transpose_unit(2)
        transpose_unit(3)
        key_stage(0)
        grouped_v = regroup_weight(raw_v, "v")
        weight_v = quantise_weight(grouped_v, "v")
        steps_per_chunk = H_TILES // STEP_TILES
        for step in range(STEPS):
            next_chunk = step // steps_per_chunk + 1
            if step % steps_per_chunk == 0 and next_chunk < CHUNKS:
                quantise_chunk(next_chunk)
            if step + 4 < UNITS:
                transpose_unit(step + 4)
            if step + 1 < STEPS:
                key_stage(step + 1)
            value_stage(step)

        results = BATCH * H_TILES
        nc.vector.tensor_reduce(
            out=totals[:, 0 : 2 * results],
            in_=parts[:].rearrange("p w (r k) -> p (w r) k", k=CHUNKS_PER_BATCH),
            axis=AXIS.X,
            op=ALU.add,
        )
        totals_bank = psum_t.tile([P, P], F32, tag="t")
        nc.tensor.transpose(totals_bank[:], totals[:], ident[:])
        rows = const.tile([P, P], F32)
        nc.vector.tensor_copy(out=rows[:], in_=totals_bank[:])
        nc.sync.dma_start(out=out_0.rearrange("n (j h) -> (n j) h", h=P), in_=rows[0:results, :])
        nc.sync.dma_start(out=out_1.rearrange("n (j h) -> (n j) h", h=P), in_=rows[results : 2 * results, :])
